import numpy as np
import ml_dtypes


def mxq(x, axis, fmt="e4m3"):
    dtype, down = {"e4m3": (ml_dtypes.float8_e4m3fn, 7), "e5m2": (ml_dtypes.float8_e5m2, 14)}[fmt]
    v = np.moveaxis(np.asarray(x, np.float32).astype(ml_dtypes.bfloat16).astype(np.float64), axis, -1)
    blocks = v.reshape(v.shape[:-1] + (-1, 32))
    amax = np.abs(blocks).max(-1, keepdims=True)
    byte = np.maximum(np.where(amax > 0, np.frexp(amax)[1] - 1 + 127, 0) - down, 1)
    scale = np.exp2(byte - 127.0)
    codes = (blocks / scale).astype(np.float32).astype(dtype).astype(np.float64)
    return np.moveaxis((codes * scale).reshape(v.shape), -1, axis)


WIDE = False


def mx_kscale(k):
    if not WIDE:
        return np.ones(k)
    levels = np.array([10, -10, 5, -5, 0])
    if k % 512:
        return np.exp2(np.random.permutation(np.resize(levels, k // 32))).repeat(32)
    a = np.empty((k // 512, 16))
    for p in range(k // 512):
        a[p, :8] = np.random.permutation(np.resize(levels, 8))
        for g in range(8):
            far = levels[np.abs(levels - a[p, g]) >= 10]
            a[p, g + 8] = far[np.random.randint(len(far))]
    return np.exp2(a.ravel()).repeat(32)


BF16 = ml_dtypes.bfloat16


def bf(x):
    return np.asarray(x, np.float32).astype(BF16)


def f64(x):
    return np.asarray(x).astype(np.float64)


B, N, C0, C1, C2, O0, O1, O2 = 16, 16, 512, 512, 512, 512, 2048, 512
G = C1 + C2
K = 2 * G


def sigmoid(v):
    return 1.0 / (1.0 + np.exp(-v))


def setup_inputs():
    s = mx_kscale(G)
    ss = np.concatenate([s, s])
    return {"x1": bf(np.random.random((B, N, C1)) * s[:C1]),
            "x2": bf(np.random.random((B, N, N, C2)) * s[C1:]),
            "W2": bf(np.random.standard_normal((K, O2)) * 2.0 / np.sqrt(K) / ss[:, None]),
            "b2": bf(np.random.standard_normal(O2) * 0.3)}


def reference(x1, x2, W2, b2):
    x1, x2 = f64(x1), f64(x2)
    e1 = np.broadcast_to(x1[:, :, None, :], (B, N, N, C1))
    g = np.concatenate([e1, x2], axis=-1)
    f2 = np.concatenate([g, np.swapaxes(g, 1, 2)], axis=-1)
    return sigmoid((mxq(f2, 3, "e4m3") @ mxq(f64(W2), 0, "e4m3")) + f64(b2))

@@ -1,0 +1,292 @@
+from contextlib import ExitStack
+
+import concourse.mybir as mybir
+from concourse.masks import make_identity
+
+F32 = mybir.dt.float32
+BF16 = mybir.dt.bfloat16
+U32 = mybir.dt.uint32
+I32 = mybir.dt.int32
+U8 = mybir.dt.uint8
+FP8X4 = mybir.dt.float8_e4m3fn_x4
+ADD = mybir.AluOpType.add
+SIGMOID = mybir.ActivationFunctionType.Sigmoid
+
+P = 128
+SCENES = 16
+OBJECTS = 16
+CHANNELS = 512
+OUT = 512
+PACK = 4
+HALVES = 2
+HALF_SCENES = SCENES // HALVES
+SCALE_WORDS = HALF_SCENES // 4
+SLAB = 4
+SLABS = OBJECTS // SLAB
+TILES = HALVES * OBJECTS
+
+W_X1_I, W_X2_IJ, W_X1_J, W_X2_JI = 0, 1, 2, 3
+
+TRANSPOSE_BANKS = 3
+TILE_BANKS = 5
+
+SWAP_PIECES = (((0, TILE_BANKS), (TILE_BANKS, OBJECTS)), ((0, SLAB), (SLAB, OBJECTS)))
+SWAP_AFTER_TILE = (7, 13)
+SECOND_X1_TERM_AFTER_TILE = 5
+
+STORE_SIZES = (4, 4, 4, 4, 4, 4, 2, 2, 2, 1, 1)
+STORE_BUFS = ((4, 5), (2, 3), (1, 2))
+
+FLOPS = 2 * SCENES * OBJECTS * OBJECTS * 4 * CHANNELS * OUT
+
+
+def tile_differentiablelogicmachine_pa_kernel(tc, x1, x2, W2, b2, out):
+    nc = tc.nc
+    with ExitStack() as ctx:
+        keep = ctx.enter_context(tc.tile_pool(name="keep", bufs=1))
+        grouped_pool = ctx.enter_context(tc.tile_pool(name="grouped", bufs=5))
+        result_pools = {}
+        for size, bufs in STORE_BUFS:
+            result_pools[size] = ctx.enter_context(tc.tile_pool(name="result%d" % size, bufs=bufs))
+        transpose_psum = ctx.enter_context(tc.psum_pool(name="transpose_psum", bufs=TRANSPOSE_BANKS))
+        tile_psum = ctx.enter_context(tc.psum_pool(name="tile_psum", bufs=TILE_BANKS))
+        ctx.enter_context(tc.manual_schedule())
+
+        identity = keep.tile([P, P], F32, name="identity")
+        ones = keep.tile([P, P], BF16, name="ones")
+        bias_row = keep.tile([P, OUT], BF16, name="bias_row")
+        bias_all = keep.tile([P, OUT], F32, name="bias_all")
+        warm = keep.tile([P, 2], F32, name="warm")
+        x1_sb = keep.tile([P, HALVES, CHANNELS], BF16, name="x1_sb")
+        x1_grouped = keep.tile([P, HALVES, P, PACK], BF16, name="x1_grouped", align_bytes=64)
+        x1_codes = keep.tile([P, HALVES, P], U32, name="x1_codes", align_bytes=64)
+        x1_scales = keep.tile([P, HALVES, P], U8, name="x1_scales", align_bytes=64)
+        w_raw = [keep.tile([P, PACK, OUT], BF16, name="w_raw%d" % g) for g in range(4)]
+        w_grouped = [keep.tile([P, OUT, PACK], BF16, name="w_grouped%d" % g, align_bytes=64) for g in range(4)]
+        w_codes = keep.tile([P, 4, OUT], U32, name="w_codes", align_bytes=64)
+        w_scales = keep.tile([P, 4, OUT], U8, name="w_scales", align_bytes=64)
+        x2_sb = [
+            [keep.tile([P, SLAB, CHANNELS], BF16, name="x2_sb%d_%d" % (h, s)) for s in range(SLABS)]
+            for h in range(HALVES)
+        ]
+
+        def operand(name):
+            codes = [keep.tile([P, OBJECTS, P], U32, name="%s_codes%d" % (name, h), align_bytes=64) for h in range(HALVES)]
+            scales = [keep.tile([P, OBJECTS, P], U8, name="%s_scales%d" % (name, h), align_bytes=64) for h in range(HALVES)]
+            return codes, scales
+
+        ij_codes, ij_scales = operand("ij")
+        ji_codes, ji_scales = operand("ji")
+        xj_codes, xj_scales = operand("xj")
+        x1_term = [keep.tile([P, OUT], F32, name="x1_term%d" % h) for h in range(HALVES)]
+
+        x1_view = x1.rearrange("(h b) i k -> h i b k", h=HALVES)
+        x2_view = x2.rearrange("(h b) i j k -> h i b (j k)", h=HALVES)
+        out_view = out.rearrange("(h b) i j o -> h i b (j o)", h=HALVES)
+        w_view = W2.rearrange("(g p t) o -> g p (t o)", g=4, t=PACK)
+
+        def load_weights(g):
+            nc.sync.dma_start(out=w_raw[g][:].rearrange("p t o -> p (t o)"), in_=w_view[g])
+
+        def load_slab(h, s):
+            nc.sync.dma_start(
+                out=x2_sb[h][s][:].rearrange("p j k -> p (j k)"),
+                in_=x2_view[h][:, :, s * SLAB * CHANNELS : (s + 1) * SLAB * CHANNELS],
+            )
+
+        nc.vector.memset(bias_row[:], 0.0)
+        for h in range(HALVES):
+            nc.sync.dma_start(out=x1_sb[:, h, :], in_=x1_view[h])
+        load_weights(W_X2_IJ)
+        load_slab(0, 0)
+        nc.sync.dma_start(out=bias_row[0:1, :], in_=b2.unsqueeze(0))
+        load_weights(W_X1_J)
+        load_slab(0, 1)
+        load_slab(0, 2)
+        load_weights(W_X2_JI)
+        load_slab(0, 3)
+        load_weights(W_X1_I)
+        for s in range(SLABS):
+            load_slab(1, s)
+
+        make_identity(nc, identity[:])
+        nc.vector.memset(ones[:], 1.0)
+        nc.vector.memset(warm[:], 0.0)
+        nc.scalar.activation(out=warm[:, 1:2], in_=warm[:, 0:1], func=SIGMOID)
+        nc.vector.memset(x1_scales[:].bitcast(I32), 0)
+        for h in range(HALVES):
+            nc.vector.memset(ij_scales[h][:].bitcast(I32), 0)
+
+        def transpose_two(rows_a, rows_b, grouped_words):
+            bank = transpose_psum.tile([P, 2, 2, P], F32, name="bank", tag="bank")
+            for block, rows in enumerate((rows_a, rows_b)):
+                for u in range(2):
+                    nc.tensor.transpose(bank[:, block, u, :], rows[:, u : 2 * P : 2], identity[:])
+            nc.scalar.copy(out=grouped_words, in_=bank[:].rearrange("p j u r -> p j r u"))
+
+        def regroup_weights(g, on_vector):
+            dst = w_grouped[g][:].rearrange("p (c i) t -> p c t i", i=4)
+            src = w_raw[g][:].rearrange("p t (c i) -> p c t i", i=4)
+            if on_vector:
+                nc.vector.tensor_copy(out=dst, in_=src)
+            else:
+                nc.scalar.copy(out=dst, in_=src)
+
+        def quantise_weights(g):
+            nc.vector.quantize_mx(
+                out=w_codes[:, g, :].bitcast(FP8X4),
+                scales=w_scales[:, g, :],
+                in_=w_grouped[g][:].rearrange("p o t -> p (o t)"),
+            )
+
+        grouped_of = {}
+
+        def transpose_slab(h, s):
+            words = x2_sb[h][s][:].bitcast(F32)
+            grouped_of[(h, s)] = grouped_pool.tile([P, SLAB, P, PACK], BF16, name="grouped", tag="grouped", align_bytes=64)
+            grouped_words = grouped_of[(h, s)][:].bitcast(F32)
+            for block in range(0, SLAB, 2):
+                transpose_two(words[:, block, :], words[:, block + 1, :], grouped_words[:, block : block + 2, :, :])
+
+        def quantise_slab(h, s):
+            blocks = slice(s * SLAB, (s + 1) * SLAB)
+            nc.vector.quantize_mx(
+                out=ij_codes[h][:, blocks, :].rearrange("p j r -> p (j r)").bitcast(FP8X4),
+                scales=ij_scales[h][:, blocks, :].rearrange("p j r -> p (j r)"),
+                in_=grouped_of[(h, s)][:].rearrange("p j r t -> p (j r t)"),
+            )
+
+        def repeat_x1(h, lo, hi):
+            for dst, src, run in ((xj_codes, x1_codes, HALF_SCENES), (xj_scales, x1_scales, SCALE_WORDS)):
+                nc.vector.tensor_copy(
+                    out=dst[h][:, lo:hi, :].bitcast(I32).rearrange("p j (i w) -> p j i w", w=run),
+                    in_=src[:, h, lo * HALF_SCENES : hi * HALF_SCENES].bitcast(I32)
+                    .rearrange("p (j w) -> p j w", w=run).unsqueeze(2).to_broadcast([P, hi - lo, OBJECTS, run]),
+                )
+
+        def swap_x2(h, lo, hi):
+            for dst, src, run in ((ji_codes, ij_codes, HALF_SCENES), (ji_scales, ij_scales, SCALE_WORDS)):
+                nc.vector.tensor_copy(
+                    out=dst[h][:, lo:hi, :].bitcast(I32).rearrange("p j (i w) -> p j i w", w=run),
+                    in_=src[h][:].bitcast(I32).rearrange("p i (j w) -> p j i w", w=run)[:, lo:hi, :, :],
+                )
+
+        def mx_pass(bank, codes, scales, g, start, stop):
+            nc.tensor.matmul_mx(
+                out=bank,
+                lhsT=codes.bitcast(FP8X4),
+                lhsT_scale=scales,
+                rhs=w_codes[:, g, :].bitcast(FP8X4),
+                rhs_scale=w_scales[:, g, :],
+                start=start,
+                stop=stop,
+            )
+
+        x1_banks = {}
+
+        def x1_term_pass(h):
+            x1_banks[h] = transpose_psum.tile([P, OUT], F32, name="x1_bank", tag="bank")
+            mx_pass(x1_banks[h][:], x1_codes[:, h, :], x1_scales[:, h, :], W_X1_I, True, True)
+
+        def x1_term_add(h):
+            nc.vector.tensor_tensor(out=x1_term[h][:], in0=x1_banks[h][:], in1=bias_all[:], op=ADD)
+
+        banks = {}
+
+        def pass_ij(n):
+            h, j = divmod(n, OBJECTS)
+            banks[n] = tile_psum.tile([P, OUT], F32, name="tile_bank", tag="tile_bank")
+            mx_pass(banks[n][:], ij_codes[h][:, j, :], ij_scales[h][:, j, :], W_X2_IJ, True, False)
+
+        def pass_xj(n):
+            h, j = divmod(n, OBJECTS)
+            mx_pass(banks[n][:], xj_codes[h][:, j, :], xj_scales[h][:, j, :], W_X1_J, False, False)
+
+        def pass_ji(n):
+            h, j = divmod(n, OBJECTS)
+            mx_pass(banks[n][:], ji_codes[h][:, j, :], ji_scales[h][:, j, :], W_X2_JI, False, True)
+
+        store_of = {}
+        first = 0
+        for size in STORE_SIZES:
+            for n in range(first, first + size):
+                store_of[n] = (first, size)
+            first += size
+        results = {}
+
+        def add_x1_term(n):
+            first_n, size = store_of[n]
+            if n == first_n:
+                results[first_n] = result_pools[size].tile([P, size, OUT], F32, name="result", tag="result")
+            nc.vector.tensor_tensor(
+                out=results[first_n][:, n - first_n, :], in0=x1_term[n // OBJECTS][:], in1=banks[n][:], op=ADD
+            )
+
+        def sigmoid_and_store(n):
+            first_n, size = store_of[n]
+            part = results[first_n][:, n - first_n, :]
+            nc.scalar.activation(out=part, in_=part, func=SIGMOID)
+            if n == first_n + size - 1:
+                h, j = divmod(n, OBJECTS)
+                nc.sync.dma_start(
+                    out=out_view[h][:, :, (j + 1 - size) * OUT : (j + 1) * OUT],
+                    in_=results[first_n][:].rearrange("p j o -> p (j o)"),
+                )
+
+        x1_words = x1_sb[:].bitcast(F32)
+        transpose_two(x1_words[:, 0, :], x1_words[:, 1, :], x1_grouped[:].bitcast(F32))
+        regroup_weights(W_X2_IJ, True)
+        nc.vector.quantize_mx(
+            out=x1_codes[:].rearrange("p h r -> p (h r)").bitcast(FP8X4),
+            scales=x1_scales[:].rearrange("p h r -> p (h r)"),
+            in_=x1_grouped[:].rearrange("p h r t -> p (h r t)"),
+        )
+        quantise_weights(W_X2_IJ)
+        regroup_weights(W_X1_J, False)
+        for h in range(HALVES):
+            repeat_x1(h, 0, OBJECTS)
+        transpose_slab(0, 0)
+        quantise_weights(W_X1_J)
+        regroup_weights(W_X2_JI, True)
+        quantise_slab(0, 0)
+        transpose_slab(0, 1)
+        quantise_weights(W_X2_JI)
+        regroup_weights(W_X1_I, True)
+        quantise_slab(0, 1)
+        transpose_slab(0, 2)
+        quantise_weights(W_X1_I)
+        quantise_slab(0, 2)
+        transpose_slab(0, 3)
+        quantise_slab(0, 3)
+        bias_bank = transpose_psum.tile([P, OUT], F32, name="bias_bank", tag="bank")
+        nc.tensor.matmul(bias_bank[:], lhsT=ones[:], rhs=bias_row[:], start=True, stop=True)
+        nc.scalar.copy(out=bias_all[:], in_=bias_bank[:])
+        for n in range(TILE_BANKS):
+            pass_ij(n)
+        for n in range(TILE_BANKS):
+            pass_xj(n)
+        x1_term_pass(0)
+        swap_x2(0, *SWAP_PIECES[0][0])
+        x1_term_add(0)
+        transpose_slab(1, 0)
+        for n in range(TILE_BANKS):
+            pass_ji(n)
+        swap_x2(0, *SWAP_PIECES[0][1])
+
+        for n in range(TILES):
+            if n + 1 < SLABS:
+                transpose_slab(1, n + 1)
+            add_x1_term(n)
+            if 1 <= n <= SLABS:
+                quantise_slab(1, n - 1)
+            if n == SECOND_X1_TERM_AFTER_TILE:
+                x1_term_pass(1)
+                x1_term_add(1)
+            if n in SWAP_AFTER_TILE:
+                swap_x2(1, *SWAP_PIECES[1][SWAP_AFTER_TILE.index(n)])
+            sigmoid_and_store(n)
+            ahead = n + TILE_BANKS
+            if ahead < TILES:
+                pass_ij(ahead)
+                pass_xj(ahead)
+                pass_ji(ahead)

@@ -53,6 +53,7 @@ def tile_differentiablelogicmachine_pa_kernel(tc, x1, x2, W2, b2, out):
         ctx.enter_context(tc.manual_schedule())
 
         identity = keep.tile([P, P], F32, name="identity")
+        reorder = keep.tile([P, P], F32, name="reorder")
         ones = keep.tile([P, P], BF16, name="ones")
         bias_row = keep.tile([P, OUT], BF16, name="bias_row")
         bias_all = keep.tile([P, OUT], F32, name="bias_all")
@@ -80,8 +81,8 @@ def tile_differentiablelogicmachine_pa_kernel(tc, x1, x2, W2, b2, out):
         xj_codes, xj_scales = operand("xj")
         x1_term = [keep.tile([P, OUT], F32, name="x1_term%d" % h) for h in range(HALVES)]
 
-        x1_view = x1.rearrange("(h b) i k -> h i b k", h=HALVES)
-        x2_view = x2.rearrange("(h b) i j k -> h i b (j k)", h=HALVES)
+        x1_view = x1.rearrange("(h b) i k -> h (b i) k", h=HALVES)
+        x2_view = x2.rearrange("(h b) i j k -> h (b i) (j k)", h=HALVES)
         out_view = out.rearrange("(h b) i j o -> h i b (j o)", h=HALVES)
         w_view = W2.rearrange("(g p t) o -> g p (t o)", g=4, t=PACK)
 
@@ -91,7 +92,7 @@ def tile_differentiablelogicmachine_pa_kernel(tc, x1, x2, W2, b2, out):
         def load_slab(h, s):
             nc.sync.dma_start(
                 out=x2_sb[h][s][:].rearrange("p j k -> p (j k)"),
-                in_=x2_view[h][:, :, s * SLAB * CHANNELS : (s + 1) * SLAB * CHANNELS],
+                in_=x2_view[h][:, s * SLAB * CHANNELS : (s + 1) * SLAB * CHANNELS],
             )
 
         nc.vector.memset(bias_row[:], 0.0)
@@ -110,6 +111,10 @@ def tile_differentiablelogicmachine_pa_kernel(tc, x1, x2, W2, b2, out):
             load_slab(1, s)
 
         make_identity(nc, identity[:])
+        nc.vector.tensor_copy(
+            out=reorder[:].rearrange("p (i b) -> p i b", b=HALF_SCENES),
+            in_=identity[:].rearrange("p (b i) -> p i b", b=HALF_SCENES),
+        )
         nc.vector.memset(ones[:], 1.0)
         nc.vector.memset(warm[:], 0.0)
         nc.scalar.activation(out=warm[:, 1:2], in_=warm[:, 0:1], func=SIGMOID)
@@ -121,7 +126,7 @@ def tile_differentiablelogicmachine_pa_kernel(tc, x1, x2, W2, b2, out):
             bank = transpose_psum.tile([P, 2, 2, P], F32, name="bank", tag="bank")
             for block, rows in enumerate((rows_a, rows_b)):
                 for u in range(2):
-                    nc.tensor.transpose(bank[:, block, u, :], rows[:, u : 2 * P : 2], identity[:])
+                    nc.tensor.transpose(bank[:, block, u, :], rows[:, u : 2 * P : 2], reorder[:])
             nc.scalar.copy(out=grouped_words, in_=bank[:].rearrange("p j u r -> p j r u"))
 
         def regroup_weights(g, on_vector):

@@ -212,8 +212,10 @@ def tile_differentiablelogicmachine_pa_kernel(tc, x1, x2, W2, b2, out):
             mx_pass(banks[n][:], ji_codes[h][:, j, :], ji_scales[h][:, j, :], W_X2_JI, False, True)
 
         store_of = {}
+        store_index = {}
         first = 0
         for size in STORE_SIZES:
+            store_index[first] = len(store_index)
             for n in range(first, first + size):
                 store_of[n] = (first, size)
             first += size
@@ -233,7 +235,8 @@ def tile_differentiablelogicmachine_pa_kernel(tc, x1, x2, W2, b2, out):
             nc.scalar.activation(out=part, in_=part, func=SIGMOID)
             if n == first_n + size - 1:
                 h, j = divmod(n, OBJECTS)
-                nc.sync.dma_start(
+                queue = (nc.sync, nc.scalar)[store_index[first_n] % 2]
+                queue.dma_start(
                     out=out_view[h][:, :, (j + 1 - size) * OUT : (j + 1) * OUT],
                     in_=results[first_n][:].rearrange("p j o -> p (j o)"),
                 )

@@ -30,11 +30,12 @@ W_X1_I, W_X2_IJ, W_X1_J, W_X2_JI = 0, 1, 2, 3
 TRANSPOSE_BANKS = 3
 TILE_BANKS = 5
 
-SWAP_PIECES = (((0, TILE_BANKS), (TILE_BANKS, OBJECTS)), ((0, SLAB), (SLAB, OBJECTS)))
+SWAP_PIECES = (((0, TILE_BANKS), (TILE_BANKS, 2 * TILE_BANKS), (2 * TILE_BANKS, OBJECTS)), ((0, SLAB), (SLAB, OBJECTS)))
 SWAP_AFTER_TILE = (7, 13)
-SECOND_X1_TERM_AFTER_TILE = 5
+SECOND_X1_PASS_AT_TILE = 6
+SECOND_X1_ADD_AT_TILE = 10
 
-STORE_SIZES = (4, 4, 4, 4, 4, 4, 2, 2, 2, 1, 1)
+STORE_SIZES = (2, 2, 4, 4, 4, 4, 4, 2, 2, 2, 1, 1)
 STORE_BUFS = ((4, 5), (2, 3), (1, 2))
 
 FLOPS = 2 * SCENES * OBJECTS * OBJECTS * 4 * CHANNELS * OUT
@@ -243,52 +244,56 @@ def tile_differentiablelogicmachine_pa_kernel(tc, x1, x2, W2, b2, out):
 
         x1_words = x1_sb[:].bitcast(F32)
         transpose_two(x1_words[:, 0, :], x1_words[:, 1, :], x1_grouped[:].bitcast(F32))
-        regroup_weights(W_X2_IJ, True)
+        regroup_weights(W_X2_IJ, False)
         nc.vector.quantize_mx(
             out=x1_codes[:].rearrange("p h r -> p (h r)").bitcast(FP8X4),
             scales=x1_scales[:].rearrange("p h r -> p (h r)"),
             in_=x1_grouped[:].rearrange("p h r t -> p (h r t)"),
         )
-        quantise_weights(W_X2_IJ)
-        regroup_weights(W_X1_J, False)
         for h in range(HALVES):
             repeat_x1(h, 0, OBJECTS)
+        quantise_weights(W_X2_IJ)
         transpose_slab(0, 0)
-        quantise_weights(W_X1_J)
-        regroup_weights(W_X2_JI, True)
+        regroup_weights(W_X1_J, False)
         quantise_slab(0, 0)
+        regroup_weights(W_X2_JI, True)
         transpose_slab(0, 1)
-        quantise_weights(W_X2_JI)
-        regroup_weights(W_X1_I, True)
+        quantise_weights(W_X1_J)
         quantise_slab(0, 1)
+        quantise_weights(W_X2_JI)
         transpose_slab(0, 2)
-        quantise_weights(W_X1_I)
+        regroup_weights(W_X1_I, True)
         quantise_slab(0, 2)
         transpose_slab(0, 3)
+        quantise_weights(W_X1_I)
         quantise_slab(0, 3)
         bias_bank = transpose_psum.tile([P, OUT], F32, name="bias_bank", tag="bank")
         nc.tensor.matmul(bias_bank[:], lhsT=ones[:], rhs=bias_row[:], start=True, stop=True)
         nc.scalar.copy(out=bias_all[:], in_=bias_bank[:])
         for n in range(TILE_BANKS):
             pass_ij(n)
+        transpose_slab(1, 0)
         for n in range(TILE_BANKS):
             pass_xj(n)
         x1_term_pass(0)
         swap_x2(0, *SWAP_PIECES[0][0])
         x1_term_add(0)
-        transpose_slab(1, 0)
         for n in range(TILE_BANKS):
             pass_ji(n)
+        transpose_slab(1, 1)
         swap_x2(0, *SWAP_PIECES[0][1])
 
         for n in range(TILES):
-            if n + 1 < SLABS:
-                transpose_slab(1, n + 1)
-            add_x1_term(n)
-            if 1 <= n <= SLABS:
-                quantise_slab(1, n - 1)
-            if n == SECOND_X1_TERM_AFTER_TILE:
+            if n + 2 < SLABS:
+                transpose_slab(1, n + 2)
+            if n == SECOND_X1_PASS_AT_TILE:
                 x1_term_pass(1)
+            add_x1_term(n)
+            if n == 0:
+                swap_x2(0, *SWAP_PIECES[0][2])
+            if 2 <= n < 2 + SLABS:
+                quantise_slab(1, n - 2)
+            if n == SECOND_X1_ADD_AT_TILE:
                 x1_term_add(1)
             if n in SWAP_AFTER_TILE:
                 swap_x2(1, *SWAP_PIECES[1][SWAP_AFTER_TILE.index(n)])

from contextlib import ExitStack

import concourse.mybir as mybir
from concourse.masks import make_identity

F32 = mybir.dt.float32
BF16 = mybir.dt.bfloat16
U32 = mybir.dt.uint32
I32 = mybir.dt.int32
U8 = mybir.dt.uint8
FP8X4 = mybir.dt.float8_e4m3fn_x4
ADD = mybir.AluOpType.add
SIGMOID = mybir.ActivationFunctionType.Sigmoid

P = 128
SCENES = 16
OBJECTS = 16
CHANNELS = 512
OUT = 512
PACK = 4
HALVES = 2
HALF_SCENES = SCENES // HALVES
SCALE_WORDS = HALF_SCENES // 4
SLAB = 4
SLABS = OBJECTS // SLAB
TILES = HALVES * OBJECTS

W_X1_I, W_X2_IJ, W_X1_J, W_X2_JI = 0, 1, 2, 3

TRANSPOSE_BANKS = 3
TILE_BANKS = 5

SWAP_PIECES = (((0, TILE_BANKS), (TILE_BANKS, 2 * TILE_BANKS), (2 * TILE_BANKS, OBJECTS)), ((0, SLAB), (SLAB, OBJECTS)))
SWAP_AFTER_TILE = (7, 13)
SECOND_X1_PASS_AT_TILE = 6
SECOND_X1_ADD_AT_TILE = 10

STORE_SIZES = (2, 2, 4, 4, 4, 4, 4, 2, 2, 2, 1, 1)
STORE_BUFS = ((4, 5), (2, 3), (1, 2))

FLOPS = 2 * SCENES * OBJECTS * OBJECTS * 4 * CHANNELS * OUT


def tile_differentiablelogicmachine_pa_kernel(tc, x1, x2, W2, b2, out):
    nc = tc.nc
    with ExitStack() as ctx:
        keep = ctx.enter_context(tc.tile_pool(name="keep", bufs=1))
        grouped_pool = ctx.enter_context(tc.tile_pool(name="grouped", bufs=5))
        result_pools = {}
        for size, bufs in STORE_BUFS:
            result_pools[size] = ctx.enter_context(tc.tile_pool(name="result%d" % size, bufs=bufs))
        transpose_psum = ctx.enter_context(tc.psum_pool(name="transpose_psum", bufs=TRANSPOSE_BANKS))
        tile_psum = ctx.enter_context(tc.psum_pool(name="tile_psum", bufs=TILE_BANKS))
        ctx.enter_context(tc.manual_schedule())

        identity = keep.tile([P, P], F32, name="identity")
        reorder = keep.tile([P, P], F32, name="reorder")
        ones = keep.tile([P, P], BF16, name="ones")
        bias_row = keep.tile([P, OUT], BF16, name="bias_row")
        bias_all = keep.tile([P, OUT], F32, name="bias_all")
        warm = keep.tile([P, 2], F32, name="warm")
        x1_sb = keep.tile([P, HALVES, CHANNELS], BF16, name="x1_sb")
        x1_grouped = keep.tile([P, HALVES, P, PACK], BF16, name="x1_grouped", align_bytes=64)
        x1_codes = keep.tile([P, HALVES, P], U32, name="x1_codes", align_bytes=64)
        x1_scales = keep.tile([P, HALVES, P], U8, name="x1_scales", align_bytes=64)
        w_raw = [keep.tile([P, PACK, OUT], BF16, name="w_raw%d" % g) for g in range(4)]
        w_grouped = [keep.tile([P, OUT, PACK], BF16, name="w_grouped%d" % g, align_bytes=64) for g in range(4)]
        w_codes = keep.tile([P, 4, OUT], U32, name="w_codes", align_bytes=64)
        w_scales = keep.tile([P, 4, OUT], U8, name="w_scales", align_bytes=64)
        x2_sb = [
            [keep.tile([P, SLAB, CHANNELS], BF16, name="x2_sb%d_%d" % (h, s)) for s in range(SLABS)]
            for h in range(HALVES)
        ]

        def operand(name):
            codes = [keep.tile([P, OBJECTS, P], U32, name="%s_codes%d" % (name, h), align_bytes=64) for h in range(HALVES)]
            scales = [keep.tile([P, OBJECTS, P], U8, name="%s_scales%d" % (name, h), align_bytes=64) for h in range(HALVES)]
            return codes, scales

        ij_codes, ij_scales = operand("ij")
        ji_codes, ji_scales = operand("ji")
        xj_codes, xj_scales = operand("xj")
        x1_term = [keep.tile([P, OUT], F32, name="x1_term%d" % h) for h in range(HALVES)]

        x1_view = x1.rearrange("(h b) i k -> h (b i) k", h=HALVES)
        x2_view = x2.rearrange("(h b) i j k -> h (b i) (j k)", h=HALVES)
        out_view = out.rearrange("(h b) i j o -> h i b (j o)", h=HALVES)
        w_view = W2.rearrange("(g p t) o -> g p (t o)", g=4, t=PACK)

        def load_weights(g):
            nc.sync.dma_start(out=w_raw[g][:].rearrange("p t o -> p (t o)"), in_=w_view[g])

        def load_slab(h, s):
            nc.sync.dma_start(
                out=x2_sb[h][s][:].rearrange("p j k -> p (j k)"),
                in_=x2_view[h][:, s * SLAB * CHANNELS : (s + 1) * SLAB * CHANNELS],
            )

        nc.vector.memset(bias_row[:], 0.0)
        for h in range(HALVES):
            nc.sync.dma_start(out=x1_sb[:, h, :], in_=x1_view[h])
        load_weights(W_X2_IJ)
        load_slab(0, 0)
        nc.sync.dma_start(out=bias_row[0:1, :], in_=b2.unsqueeze(0))
        load_weights(W_X1_J)
        load_slab(0, 1)
        load_slab(0, 2)
        load_weights(W_X2_JI)
        load_slab(0, 3)
        load_weights(W_X1_I)
        for s in range(SLABS):
            load_slab(1, s)

        make_identity(nc, identity[:])
        nc.vector.tensor_copy(
            out=reorder[:].rearrange("p (i b) -> p i b", b=HALF_SCENES),
            in_=identity[:].rearrange("p (b i) -> p i b", b=HALF_SCENES),
        )
        nc.vector.memset(ones[:], 1.0)
        nc.vector.memset(warm[:], 0.0)
        nc.scalar.activation(out=warm[:, 1:2], in_=warm[:, 0:1], func=SIGMOID)
        nc.vector.memset(x1_scales[:].bitcast(I32), 0)
        for h in range(HALVES):
            nc.vector.memset(ij_scales[h][:].bitcast(I32), 0)

        def transpose_two(rows_a, rows_b, grouped_words):
            bank = transpose_psum.tile([P, 2, 2, P], F32, name="bank", tag="bank")
            for block, rows in enumerate((rows_a, rows_b)):
                for u in range(2):
                    nc.tensor.transpose(bank[:, block, u, :], rows[:, u : 2 * P : 2], reorder[:])
            nc.scalar.copy(out=grouped_words, in_=bank[:].rearrange("p j u r -> p j r u"))

        def regroup_weights(g, on_vector):
            dst = w_grouped[g][:].rearrange("p (c i) t -> p c t i", i=4)
            src = w_raw[g][:].rearrange("p t (c i) -> p c t i", i=4)
            if on_vector:
                nc.vector.tensor_copy(out=dst, in_=src)
            else:
                nc.scalar.copy(out=dst, in_=src)

        def quantise_weights(g):
            nc.vector.quantize_mx(
                out=w_codes[:, g, :].bitcast(FP8X4),
                scales=w_scales[:, g, :],
                in_=w_grouped[g][:].rearrange("p o t -> p (o t)"),
            )

        grouped_of = {}

        def transpose_slab(h, s):
            words = x2_sb[h][s][:].bitcast(F32)
            grouped_of[(h, s)] = grouped_pool.tile([P, SLAB, P, PACK], BF16, name="grouped", tag="grouped", align_bytes=64)
            grouped_words = grouped_of[(h, s)][:].bitcast(F32)
            for block in range(0, SLAB, 2):
                transpose_two(words[:, block, :], words[:, block + 1, :], grouped_words[:, block : block + 2, :, :])

        def quantise_slab(h, s):
            blocks = slice(s * SLAB, (s + 1) * SLAB)
            nc.vector.quantize_mx(
                out=ij_codes[h][:, blocks, :].rearrange("p j r -> p (j r)").bitcast(FP8X4),
                scales=ij_scales[h][:, blocks, :].rearrange("p j r -> p (j r)"),
                in_=grouped_of[(h, s)][:].rearrange("p j r t -> p (j r t)"),
            )

        def repeat_x1(h, lo, hi):
            for dst, src, run in ((xj_codes, x1_codes, HALF_SCENES), (xj_scales, x1_scales, SCALE_WORDS)):
                nc.vector.tensor_copy(
                    out=dst[h][:, lo:hi, :].bitcast(I32).rearrange("p j (i w) -> p j i w", w=run),
                    in_=src[:, h, lo * HALF_SCENES : hi * HALF_SCENES].bitcast(I32)
                    .rearrange("p (j w) -> p j w", w=run).unsqueeze(2).to_broadcast([P, hi - lo, OBJECTS, run]),
                )

        def swap_x2(h, lo, hi):
            for dst, src, run in ((ji_codes, ij_codes, HALF_SCENES), (ji_scales, ij_scales, SCALE_WORDS)):
                nc.vector.tensor_copy(
                    out=dst[h][:, lo:hi, :].bitcast(I32).rearrange("p j (i w) -> p j i w", w=run),
                    in_=src[h][:].bitcast(I32).rearrange("p i (j w) -> p j i w", w=run)[:, lo:hi, :, :],
                )

        def mx_pass(bank, codes, scales, g, start, stop):
            nc.tensor.matmul_mx(
                out=bank,
                lhsT=codes.bitcast(FP8X4),
                lhsT_scale=scales,
                rhs=w_codes[:, g, :].bitcast(FP8X4),
                rhs_scale=w_scales[:, g, :],
                start=start,
                stop=stop,
            )

        x1_banks = {}

        def x1_term_pass(h):
            x1_banks[h] = transpose_psum.tile([P, OUT], F32, name="x1_bank", tag="bank")
            mx_pass(x1_banks[h][:], x1_codes[:, h, :], x1_scales[:, h, :], W_X1_I, True, True)

        def x1_term_add(h):
            nc.vector.tensor_tensor(out=x1_term[h][:], in0=x1_banks[h][:], in1=bias_all[:], op=ADD)

        banks = {}

        def pass_ij(n):
            h, j = divmod(n, OBJECTS)
            banks[n] = tile_psum.tile([P, OUT], F32, name="tile_bank", tag="tile_bank")
            mx_pass(banks[n][:], ij_codes[h][:, j, :], ij_scales[h][:, j, :], W_X2_IJ, True, False)

        def pass_xj(n):
            h, j = divmod(n, OBJECTS)
            mx_pass(banks[n][:], xj_codes[h][:, j, :], xj_scales[h][:, j, :], W_X1_J, False, False)

        def pass_ji(n):
            h, j = divmod(n, OBJECTS)
            mx_pass(banks[n][:], ji_codes[h][:, j, :], ji_scales[h][:, j, :], W_X2_JI, False, True)

        store_of = {}
        store_index = {}
        first = 0
        for size in STORE_SIZES:
            store_index[first] = len(store_index)
            for n in range(first, first + size):
                store_of[n] = (first, size)
            first += size
        results = {}

        def add_x1_term(n):
            first_n, size = store_of[n]
            if n == first_n:
                results[first_n] = result_pools[size].tile([P, size, OUT], F32, name="result", tag="result")
            nc.vector.tensor_tensor(
                out=results[first_n][:, n - first_n, :], in0=x1_term[n // OBJECTS][:], in1=banks[n][:], op=ADD
            )

        def sigmoid_and_store(n):
            first_n, size = store_of[n]
            part = results[first_n][:, n - first_n, :]
            nc.scalar.activation(out=part, in_=part, func=SIGMOID)
            if n == first_n + size - 1:
                h, j = divmod(n, OBJECTS)
                queue = (nc.sync, nc.scalar)[store_index[first_n] % 2]
                queue.dma_start(
                    out=out_view[h][:, :, (j + 1 - size) * OUT : (j + 1) * OUT],
                    in_=results[first_n][:].rearrange("p j o -> p (j o)"),
                )

        x1_words = x1_sb[:].bitcast(F32)
        transpose_two(x1_words[:, 0, :], x1_words[:, 1, :], x1_grouped[:].bitcast(F32))
        regroup_weights(W_X2_IJ, False)
        nc.vector.quantize_mx(
            out=x1_codes[:].rearrange("p h r -> p (h r)").bitcast(FP8X4),
            scales=x1_scales[:].rearrange("p h r -> p (h r)"),
            in_=x1_grouped[:].rearrange("p h r t -> p (h r t)"),
        )
        for h in range(HALVES):
            repeat_x1(h, 0, OBJECTS)
        quantise_weights(W_X2_IJ)
        transpose_slab(0, 0)
        regroup_weights(W_X1_J, False)
        quantise_slab(0, 0)
        regroup_weights(W_X2_JI, True)
        transpose_slab(0, 1)
        quantise_weights(W_X1_J)
        quantise_slab(0, 1)
        quantise_weights(W_X2_JI)
        transpose_slab(0, 2)
        regroup_weights(W_X1_I, True)
        quantise_slab(0, 2)
        transpose_slab(0, 3)
        quantise_weights(W_X1_I)
        quantise_slab(0, 3)
        bias_bank = transpose_psum.tile([P, OUT], F32, name="bias_bank", tag="bank")
        nc.tensor.matmul(bias_bank[:], lhsT=ones[:], rhs=bias_row[:], start=True, stop=True)
        nc.scalar.copy(out=bias_all[:], in_=bias_bank[:])
        for n in range(TILE_BANKS):
            pass_ij(n)
        transpose_slab(1, 0)
        for n in range(TILE_BANKS):
            pass_xj(n)
        x1_term_pass(0)
        swap_x2(0, *SWAP_PIECES[0][0])
        x1_term_add(0)
        for n in range(TILE_BANKS):
            pass_ji(n)
        transpose_slab(1, 1)
        swap_x2(0, *SWAP_PIECES[0][1])

        for n in range(TILES):
            if n + 2 < SLABS:
                transpose_slab(1, n + 2)
            if n == SECOND_X1_PASS_AT_TILE:
                x1_term_pass(1)
            add_x1_term(n)
            if n == 0:
                swap_x2(0, *SWAP_PIECES[0][2])
            if 2 <= n < 2 + SLABS:
                quantise_slab(1, n - 2)
            if n == SECOND_X1_ADD_AT_TILE:
                x1_term_add(1)
            if n in SWAP_AFTER_TILE:
                swap_x2(1, *SWAP_PIECES[1][SWAP_AFTER_TILE.index(n)])
            sigmoid_and_store(n)
            ahead = n + TILE_BANKS
            if ahead < TILES:
                pass_ij(ahead)
                pass_xj(ahead)
                pass_ji(ahead)
